import numpy as np
import ml_dtypes


def mxq(x, axis, fmt="e4m3"):
    dtype, down = {"e4m3": (ml_dtypes.float8_e4m3fn, 7), "e5m2": (ml_dtypes.float8_e5m2, 14)}[fmt]
    v = np.moveaxis(np.asarray(x, np.float32).astype(ml_dtypes.bfloat16).astype(np.float64), axis, -1)
    blocks = v.reshape(v.shape[:-1] + (-1, 32))
    amax = np.abs(blocks).max(-1, keepdims=True)
    byte = np.maximum(np.where(amax > 0, np.frexp(amax)[1] - 1 + 127, 0) - down, 1)
    scale = np.exp2(byte - 127.0)
    codes = (blocks / scale).astype(np.float32).astype(dtype).astype(np.float64)
    return np.moveaxis((codes * scale).reshape(v.shape), -1, axis)


WIDE = False


def mx_kscale(k):
    if not WIDE:
        return np.ones(k)
    levels = np.array([10, -10, 5, -5, 0])
    if k % 512:
        return np.exp2(np.random.permutation(np.resize(levels, k // 32))).repeat(32)
    a = np.empty((k // 512, 16))
    for p in range(k // 512):
        a[p, :8] = np.random.permutation(np.resize(levels, 8))
        for g in range(8):
            far = levels[np.abs(levels - a[p, g]) >= 10]
            a[p, g + 8] = far[np.random.randint(len(far))]
    return np.exp2(a.ravel()).repeat(32)


BF16 = ml_dtypes.bfloat16


def bf(x):
    return np.asarray(x, np.float32).astype(BF16)


def f64(x):
    return np.asarray(x).astype(np.float64)


N, IN_DIM, HID, OUT_DIM = 1024, 1024, 512, 256
CAT = 3 * HID


def log_softmax(v):
    d = v - v.max(-1, keepdims=True)
    return d - np.log(np.exp(d).sum(-1, keepdims=True))


def setup_inputs():
    s, t = mx_kscale(HID), mx_kscale(CAT)
    ta, tb, tc = t[:HID], t[HID:2 * HID], t[2 * HID:]
    return {"u1": bf(np.maximum(np.random.standard_normal((N, HID)) * 2.0, 0.0) * s),
            "W2_1": bf(np.random.standard_normal((HID, HID)) * 0.5 / np.sqrt(HID) / s[:, None] * tc),
            "b2_1": bf(np.random.standard_normal(HID) * 0.3 * tc),
            "h": bf(np.random.standard_normal((N, HID)) * ta),
            "h1": bf(np.random.standard_normal((N, HID)) * 0.8 * tb),
            "W_out": bf(np.random.standard_normal((CAT, OUT_DIM)) * 2.0 / np.sqrt(CAT) / t[:, None]),
            "b_out": bf(np.random.standard_normal(OUT_DIM) * 0.3)}


def reference(u1, W2_1, b2_1, h, h1, W_out, b_out):
    h2 = (mxq(f64(u1), 1, "e4m3") @ mxq(f64(W2_1), 0, "e4m3")) + f64(b2_1)
    cat = np.concatenate([f64(h), f64(h1), h2], axis=-1)
    logits = (mxq(cat, 1, "e4m3") @ mxq(f64(W_out), 0, "e4m3")) + f64(b_out)
    return log_softmax(logits)

@@ -1,0 +1,270 @@
+from contextlib import ExitStack
+
+import concourse.mybir as mybir
+from concourse.masks import make_identity
+
+F32 = mybir.dt.float32
+BF16 = mybir.dt.bfloat16
+U32 = mybir.dt.uint32
+U8 = mybir.dt.uint8
+FP8X4 = mybir.dt.float8_e4m3fn_x4
+ACT = mybir.ActivationFunctionType
+ALU = mybir.AluOpType
+AX = mybir.AxisListType
+
+NODES, HID, CLASSES = 1024, 512, 256
+FLOPS = 2 * NODES * HID * HID + 2 * NODES * 3 * HID * CLASSES
+
+P = 128
+PACK = 4
+TILES = NODES // P
+UNITS = TILES // 2
+STAGE1_PSUM = F32
+W2_HALF = HID // 2 // PACK
+W2_ON_VECTOR = 40
+
+
+def tile_gin_pc_kernel(tc, u1, W2_1, b2_1, h, h1, W_out, b_out, out):
+    nc = tc.nc
+    with ExitStack() as ctx:
+        keep = ctx.enter_context(tc.tile_pool(name="keep", bufs=1))
+        psum = ctx.enter_context(tc.psum_pool(name="psum", bufs=1))
+        ctx.enter_context(tc.manual_schedule())
+
+        ident = keep.tile([P, P], F32, name="ident")
+        make_identity(nc, ident[:])
+        ones = keep.tile([P, P], BF16, name="ones")
+        nc.vector.memset(ones[:], 1.0)
+        b_out_row = keep.tile([P, CLASSES], BF16, name="b_out_row")
+        nc.vector.memset(b_out_row[:], 0.0)
+        warm = keep.tile([P, 2], F32, name="warm")
+        nc.vector.memset(warm[:], 0.0)
+        nc.scalar.activation(out=warm[:, 1:2], in_=warm[:, 0:1], func=ACT.Exp)
+
+        sources = {"u1": u1, "h": h, "h1": h1}
+        raw = {}
+        for name in sources:
+            for j in range(UNITS):
+                raw[(name, j)] = keep.tile([P, 2, HID], BF16, name="raw_%s_%d" % (name, j))
+        w2_raw = [keep.tile([P, PACK, HID // 2], BF16, name="w2_raw%d" % a) for a in range(2)]
+        wo_raw = [keep.tile([P, PACK, CLASSES], BF16, name="wo_raw%d" % g) for g in range(3)]
+        b2 = keep.tile([P, PACK], BF16, name="b2")
+        b_out_all = keep.tile([P, CLASSES], F32, name="b_out_all")
+
+        w2_in = keep.tile([P, PACK * HID], BF16, name="w2_in", align_bytes=64)
+        w2_codes = keep.tile([P, HID], U32, name="w2_codes", align_bytes=64)
+        w2_scales = keep.tile([P, HID], U8, name="w2_scales", align_bytes=64)
+        wo_in = keep.tile([P, 3 * PACK * CLASSES], BF16, name="wo_in", align_bytes=64)
+        wo_codes = keep.tile([P, 3 * CLASSES], U32, name="wo_codes", align_bytes=64)
+        wo_scales = keep.tile([P, 3 * CLASSES], U8, name="wo_scales", align_bytes=64)
+        u1_in = [keep.tile([P, 2 * P * PACK], BF16, name="u1_in%d" % j, align_bytes=64) for j in range(UNITS)]
+        u1_codes = [keep.tile([P, 2 * P], U32, name="u1_codes%d" % j, align_bytes=64) for j in range(UNITS)]
+        u1_scales = [keep.tile([P, 2 * P], U8, name="u1_scales%d" % j, align_bytes=64) for j in range(UNITS)]
+        hh_in = [keep.tile([P, 2, 2 * P * PACK], BF16, name="hh_in%d" % j, align_bytes=64) for j in range(UNITS)]
+        hh_codes = [keep.tile([P, 4 * P], U32, name="hh_codes%d" % j, align_bytes=64) for j in range(UNITS)]
+        hh_scales = [keep.tile([P, 4 * P], U8, name="hh_scales%d" % j, align_bytes=64) for j in range(UNITS)]
+        h2_in = [keep.tile([P, 2, P * PACK], BF16, name="h2_in%d" % j, align_bytes=64) for j in range(UNITS)]
+        h2_codes = [keep.tile([P, 2 * P], U32, name="h2_codes%d" % j, align_bytes=64) for j in range(UNITS)]
+        h2_scales = [keep.tile([P, 2 * P], U8, name="h2_scales%d" % j, align_bytes=64) for j in range(UNITS)]
+
+        logits = [keep.tile([P, 2, CLASSES], F32, name="logits%d" % j) for j in range(UNITS)]
+        result = [keep.tile([P, 2, CLASSES], F32, name="result%d" % j) for j in range(UNITS)]
+        neg_max = keep.tile([P, TILES], F32, name="neg_max")
+        exp_sum = keep.tile([P, TILES], F32, name="exp_sum")
+        log_sum = keep.tile([P, TILES], F32, name="log_sum")
+        exp_values = keep.tile([P, CLASSES], BF16, name="exp_values")
+
+        banks = {}
+
+        def load_nodes(name, j):
+            view = sources[name].rearrange("(p i) k -> p i k", i=TILES)
+            nc.sync.dma_start(out=raw[(name, j)][:], in_=view[:, 2 * j:2 * j + 2, :])
+
+        def load_w2(a):
+            view = W2_1.rearrange("(p t) c -> p t c", t=PACK)
+            nc.sync.dma_start(out=w2_raw[a][:], in_=view[:, :, 256 * a:256 * (a + 1)])
+
+        def load_wo(g):
+            rows = W_out[HID * g:HID * (g + 1), :]
+            nc.sync.dma_start(out=wo_raw[g][:], in_=rows.rearrange("(p t) c -> p t c", t=PACK))
+
+        def load_biases():
+            nc.sync.dma_start(out=b2[:], in_=b2_1.rearrange("(p t) -> p t", t=PACK))
+            nc.sync.dma_start(out=b_out_row[0:1, :], in_=b_out.unsqueeze(0))
+
+        def interleave_w2(a):
+            dst = w2_in[:].rearrange("p (s m t) -> p s m t", s=PACK, t=PACK)
+            src = w2_raw[a][:].rearrange("p t (m s) -> p s m t", s=PACK)
+            m0 = W2_HALF * a
+            nc.vector.tensor_copy(out=dst[:, :, m0:m0 + W2_ON_VECTOR, :], in_=src[:, :, 0:W2_ON_VECTOR, :])
+            nc.scalar.copy(out=dst[:, :, m0 + W2_ON_VECTOR:m0 + W2_HALF, :], in_=src[:, :, W2_ON_VECTOR:W2_HALF, :])
+
+        def quantize_w2():
+            nc.vector.quantize_mx(out=w2_codes[:].bitcast(FP8X4), scales=w2_scales[:], in_=w2_in[:])
+
+        def interleave_wo(g):
+            width = PACK * CLASSES
+            nc.scalar.copy(out=wo_in[:, width * g:width * (g + 1)].rearrange("p (c t) -> p c t", t=PACK),
+                           in_=wo_raw[g][:].rearrange("p t c -> p c t"))
+
+        def quantize_wo(g0, g1):
+            nc.vector.quantize_mx(out=wo_codes[:, CLASSES * g0:CLASSES * g1].bitcast(FP8X4),
+                                  scales=wo_scales[:, CLASSES * g0:CLASSES * g1],
+                                  in_=wo_in[:, PACK * CLASSES * g0:PACK * CLASSES * g1])
+
+        def spread_b_out():
+            bank = psum.tile([P, 2, CLASSES], F32, name="spread", tag="logits", bufs=2)
+            nc.tensor.matmul(out=bank[:, 0, :], lhsT=ones[:], rhs=b_out_row[:], start=True, stop=True)
+            nc.scalar.copy(out=b_out_all[:], in_=bank[:, 0, :])
+
+        def transpose(name, j):
+            words = raw[(name, j)][:].bitcast(F32)
+            bank = psum.tile([P, 2, 2, P], F32, name="turned", tag="turned", bufs=4)
+            banks[(name, j)] = bank
+            for i in range(2):
+                for u in range(2):
+                    nc.tensor.transpose(bank[:, i, u, :], words[:, i, u:HID // 2:2], ident[:])
+
+        def copy_out(name, j):
+            dst = u1_in[j][:] if name == "u1" else hh_in[j][:, 0 if name == "h" else 1, :]
+            nc.scalar.copy(out=dst.bitcast(F32).rearrange("p (i r u) -> p i r u", i=2, u=2),
+                           in_=banks[(name, j)][:].rearrange("p i u r -> p i r u"))
+
+        def quantize_u1(j):
+            nc.vector.quantize_mx(out=u1_codes[j][:].bitcast(FP8X4), scales=u1_scales[j][:], in_=u1_in[j][:])
+
+        def quantize_hh(j):
+            nc.vector.quantize_mx(out=hh_codes[j][:].bitcast(FP8X4), scales=hh_scales[j][:],
+                                  in_=hh_in[j][:].rearrange("p x c -> p (x c)"))
+
+        def stage1_matmuls(tile):
+            j, i = tile // 2, tile % 2
+            nodes = slice(P * i, P * (i + 1))
+            bank = psum.tile([P, PACK, P], STAGE1_PSUM, name="stage1", tag="stage1", bufs=2)
+            banks[("h2", tile)] = bank
+            for s in range(PACK):
+                block = slice(P * s, P * (s + 1))
+                nc.tensor.matmul_mx(out=bank[:, s, :],
+                                    lhsT=w2_codes[:, block].bitcast(FP8X4), lhsT_scale=w2_scales[:, block],
+                                    rhs=u1_codes[j][:, nodes].bitcast(FP8X4), rhs_scale=u1_scales[j][:, nodes],
+                                    start=True, stop=True)
+
+        def stage1_bias(tile):
+            j, i = tile // 2, tile % 2
+            nc.vector.tensor_tensor(out=h2_in[j][:, i, :].rearrange("p (n s) -> p n s", s=PACK),
+                                    in0=banks[("h2", tile)][:].rearrange("p s n -> p n s"),
+                                    in1=b2[:].unsqueeze(1).to_broadcast([P, P, PACK]), op=ALU.add)
+
+        def quantize_h2(j):
+            nc.vector.quantize_mx(out=h2_codes[j][:].bitcast(FP8X4), scales=h2_scales[j][:],
+                                  in_=h2_in[j][:].rearrange("p i c -> p (i c)"))
+
+        def stage2_matmuls(j):
+            bank = psum.tile([P, 2, CLASSES], F32, name="logits", tag="logits", bufs=2)
+            banks[("logits", j)] = bank
+            for i in range(2):
+                passes = ((hh_codes[j], hh_scales[j], P * i),
+                          (hh_codes[j], hh_scales[j], 2 * P + P * i),
+                          (h2_codes[j], h2_scales[j], P * i))
+                for g in range(3):
+                    codes, scales, first = passes[g]
+                    nc.tensor.matmul_mx(out=bank[:, i, :],
+                                        lhsT=codes[:, first:first + P].bitcast(FP8X4),
+                                        lhsT_scale=scales[:, first:first + P],
+                                        rhs=wo_codes[:, CLASSES * g:CLASSES * (g + 1)].bitcast(FP8X4),
+                                        rhs_scale=wo_scales[:, CLASSES * g:CLASSES * (g + 1)],
+                                        start=(g == 0), stop=(g == 2))
+
+        def add_b_out(j):
+            nc.vector.tensor_tensor(out=logits[j][:], in0=banks[("logits", j)][:],
+                                    in1=b_out_all[:].unsqueeze(1).to_broadcast([P, 2, CLASSES]), op=ALU.add)
+
+        def row_max(first, last):
+            j = first // 2
+            nc.vector.tensor_reduce(out=neg_max[:, first:last], in_=logits[j][:, first - 2 * j:last - 2 * j, :],
+                                    axis=AX.X, op=ALU.max, negate=True)
+
+        def exp_and_sum(tile):
+            nc.scalar.activation(out=exp_values[:], in_=logits[tile // 2][:, tile % 2, :], func=ACT.Exp,
+                                 bias=neg_max[:, tile:tile + 1], scale=1.0, accum_out=exp_sum[:, tile:tile + 1])
+
+        def subtract(tile):
+            nc.vector.tensor_scalar(out=result[tile // 2][:, tile % 2, :], in0=logits[tile // 2][:, tile % 2, :],
+                                    scalar1=neg_max[:, tile:tile + 1], scalar2=log_sum[:, tile:tile + 1],
+                                    op0=ALU.add, op1=ALU.subtract)
+
+        def store(j):
+            view = out.rearrange("(p i) c -> p i c", i=TILES)
+            nc.sync.dma_start(out=view[:, 2 * j:2 * j + 2, :], in_=result[j][:])
+
+        load_nodes("u1", 0)
+        load_w2(0)
+        load_nodes("u1", 1)
+        load_w2(1)
+        load_nodes("u1", 2)
+        load_biases()
+        load_nodes("u1", 3)
+        load_wo(0)
+        load_wo(1)
+        load_nodes("h", 0)
+        load_nodes("h1", 0)
+        load_wo(2)
+        for j in range(1, UNITS):
+            load_nodes("h", j)
+            load_nodes("h1", j)
+
+        transpose("u1", 0)
+        interleave_w2(0)
+        copy_out("u1", 0)
+        interleave_w2(1)
+        quantize_u1(0)
+        quantize_w2()
+        for j in (1, 2):
+            transpose("u1", j)
+            copy_out("u1", j)
+            quantize_u1(j)
+        spread_b_out()
+        transpose("u1", 3)
+        copy_out("u1", 3)
+
+        for j in range(UNITS):
+            stage1_matmuls(2 * j)
+            stage1_matmuls(2 * j + 1)
+            transpose("h", j)
+            transpose("h1", j)
+            stage1_bias(2 * j)
+            stage1_bias(2 * j + 1)
+            if j == 0:
+                quantize_u1(3)
+                interleave_wo(0)
+                interleave_wo(1)
+            elif j == 1:
+                quantize_wo(0, 2)
+                interleave_wo(2)
+            elif j == 2:
+                quantize_wo(2, 3)
+            else:
+                quantize_hh(0)
+            quantize_h2(j)
+            copy_out("h", j)
+            copy_out("h1", j)
+
+        quantize_hh(1)
+        for j in range(UNITS):
+            stage2_matmuls(j)
+            if j + 2 < UNITS:
+                quantize_hh(j + 2)
+            if j > 0:
+                row_max(2 * j - 2, 2 * j)
+                exp_and_sum(2 * j - 2)
+                exp_and_sum(2 * j - 1)
+            add_b_out(j)
+        for tile in (TILES - 2, TILES - 1):
+            row_max(tile, tile + 1)
+            exp_and_sum(tile)
+
+        nc.scalar.activation(out=log_sum[:], in_=exp_sum[:], func=ACT.Ln)
+        for j in range(UNITS):
+            subtract(2 * j)
+            subtract(2 * j + 1)
+            store(j)

@@ -37,6 +37,8 @@ def tile_gin_pc_kernel(tc, u1, W2_1, b2_1, h, h1, W_out, b_out, out):
         nc.vector.memset(ones[:], 1.0)
         b_out_row = keep.tile([P, CLASSES], BF16, name="b_out_row")
         nc.vector.memset(b_out_row[:], 0.0)
+        ones_wide = keep.tile([P, HID], BF16, name="ones_wide")
+        nc.vector.memset(ones_wide[:], 1.0)
         warm = keep.tile([P, 2], F32, name="warm")
         nc.vector.memset(warm[:], 0.0)
         nc.scalar.activation(out=warm[:, 1:2], in_=warm[:, 0:1], func=ACT.Exp)
@@ -75,6 +77,17 @@ def tile_gin_pc_kernel(tc, u1, W2_1, b2_1, h, h1, W_out, b_out, out):
         exp_values = keep.tile([P, CLASSES], BF16, name="exp_values")
 
         banks = {}
+
+        spare = psum.tile([P, 2, CLASSES], F32, name="spare", tag="logits", bufs=2)
+
+        def spare_plain_pass():
+            nc.tensor.matmul(out=spare[:].rearrange("p a c -> p (a c)"), lhsT=ones[:], rhs=ones_wide[:],
+                             start=True, stop=True)
+
+        def spare_mx_pass():
+            nc.tensor.matmul_mx(out=spare[:].rearrange("p a c -> p (a c)"),
+                                lhsT=w2_codes[:, 0:P].bitcast(FP8X4), lhsT_scale=w2_scales[:, 0:P],
+                                rhs=w2_codes[:].bitcast(FP8X4), rhs_scale=w2_scales[:], start=True, stop=True)
 
         def load_nodes(name, j):
             view = sources[name].rearrange("(p i) k -> p i k", i=TILES)
@@ -213,7 +226,10 @@ def tile_gin_pc_kernel(tc, u1, W2_1, b2_1, h, h1, W_out, b_out, out):
             load_nodes("h", j)
             load_nodes("h1", j)
 
+        for n in range(4):
+            spare_plain_pass()
         transpose("u1", 0)
+        spare_plain_pass()
         interleave_w2(0)
         copy_out("u1", 0)
         interleave_w2(1)
@@ -221,15 +237,19 @@ def tile_gin_pc_kernel(tc, u1, W2_1, b2_1, h, h1, W_out, b_out, out):
         quantize_w2()
         for j in (1, 2):
             transpose("u1", j)
+            if j == 1:
+                spare_plain_pass()
             copy_out("u1", j)
             quantize_u1(j)
         spread_b_out()
+        spare_plain_pass()
         transpose("u1", 3)
         copy_out("u1", 3)
 
         for j in range(UNITS):
             stage1_matmuls(2 * j)
             stage1_matmuls(2 * j + 1)
+            spare_mx_pass()
             transpose("h", j)
             transpose("h1", j)
             stage1_bias(2 * j)
@@ -249,6 +269,8 @@ def tile_gin_pc_kernel(tc, u1, W2_1, b2_1, h, h1, W_out, b_out, out):
             copy_out("h", j)
             copy_out("h1", j)
 
+        spare_mx_pass()
+        spare_mx_pass()
         quantize_hh(1)
         for j in range(UNITS):
             stage2_matmuls(j)

@@ -20,8 +20,8 @@ PACK = 4
 TILES = NODES // P
 UNITS = TILES // 2
 STAGE1_PSUM = F32
-W2_HALF = HID // 2 // PACK
-W2_ON_VECTOR = 40
+W2_ON_VECTOR = 84
+EARLY_TILES = 4
 
 
 def tile_gin_pc_kernel(tc, u1, W2_1, b2_1, h, h1, W_out, b_out, out):
@@ -37,8 +37,6 @@ def tile_gin_pc_kernel(tc, u1, W2_1, b2_1, h, h1, W_out, b_out, out):
         nc.vector.memset(ones[:], 1.0)
         b_out_row = keep.tile([P, CLASSES], BF16, name="b_out_row")
         nc.vector.memset(b_out_row[:], 0.0)
-        ones_wide = keep.tile([P, HID], BF16, name="ones_wide")
-        nc.vector.memset(ones_wide[:], 1.0)
         warm = keep.tile([P, 2], F32, name="warm")
         nc.vector.memset(warm[:], 0.0)
         nc.scalar.activation(out=warm[:, 1:2], in_=warm[:, 0:1], func=ACT.Exp)
@@ -48,7 +46,7 @@ def tile_gin_pc_kernel(tc, u1, W2_1, b2_1, h, h1, W_out, b_out, out):
         for name in sources:
             for j in range(UNITS):
                 raw[(name, j)] = keep.tile([P, 2, HID], BF16, name="raw_%s_%d" % (name, j))
-        w2_raw = [keep.tile([P, PACK, HID // 2], BF16, name="w2_raw%d" % a) for a in range(2)]
+        w2_raw = keep.tile([P, PACK, HID], BF16, name="w2_raw")
         wo_raw = [keep.tile([P, PACK, CLASSES], BF16, name="wo_raw%d" % g) for g in range(3)]
         b2 = keep.tile([P, PACK], BF16, name="b2")
         b_out_all = keep.tile([P, CLASSES], F32, name="b_out_all")
@@ -78,24 +76,12 @@ def tile_gin_pc_kernel(tc, u1, W2_1, b2_1, h, h1, W_out, b_out, out):
 
         banks = {}
 
-        spare = psum.tile([P, 2, CLASSES], F32, name="spare", tag="logits", bufs=2)
-
-        def spare_plain_pass():
-            nc.tensor.matmul(out=spare[:].rearrange("p a c -> p (a c)"), lhsT=ones[:], rhs=ones_wide[:],
-                             start=True, stop=True)
-
-        def spare_mx_pass():
-            nc.tensor.matmul_mx(out=spare[:].rearrange("p a c -> p (a c)"),
-                                lhsT=w2_codes[:, 0:P].bitcast(FP8X4), lhsT_scale=w2_scales[:, 0:P],
-                                rhs=w2_codes[:].bitcast(FP8X4), rhs_scale=w2_scales[:], start=True, stop=True)
-
         def load_nodes(name, j):
             view = sources[name].rearrange("(p i) k -> p i k", i=TILES)
             nc.sync.dma_start(out=raw[(name, j)][:], in_=view[:, 2 * j:2 * j + 2, :])
 
-        def load_w2(a):
-            view = W2_1.rearrange("(p t) c -> p t c", t=PACK)
-            nc.sync.dma_start(out=w2_raw[a][:], in_=view[:, :, 256 * a:256 * (a + 1)])
+        def load_w2():
+            nc.sync.dma_start(out=w2_raw[:], in_=W2_1.rearrange("(p t) c -> p t c", t=PACK))
 
         def load_wo(g):
             rows = W_out[HID * g:HID * (g + 1), :]
@@ -105,12 +91,11 @@ def tile_gin_pc_kernel(tc, u1, W2_1, b2_1, h, h1, W_out, b_out, out):
             nc.sync.dma_start(out=b2[:], in_=b2_1.rearrange("(p t) -> p t", t=PACK))
             nc.sync.dma_start(out=b_out_row[0:1, :], in_=b_out.unsqueeze(0))
 
-        def interleave_w2(a):
+        def interleave_w2():
             dst = w2_in[:].rearrange("p (s m t) -> p s m t", s=PACK, t=PACK)
-            src = w2_raw[a][:].rearrange("p t (m s) -> p s m t", s=PACK)
-            m0 = W2_HALF * a
-            nc.vector.tensor_copy(out=dst[:, :, m0:m0 + W2_ON_VECTOR, :], in_=src[:, :, 0:W2_ON_VECTOR, :])
-            nc.scalar.copy(out=dst[:, :, m0 + W2_ON_VECTOR:m0 + W2_HALF, :], in_=src[:, :, W2_ON_VECTOR:W2_HALF, :])
+            src = w2_raw[:].rearrange("p t (m s) -> p s m t", s=PACK)
+            nc.vector.tensor_copy(out=dst[:, :, 0:W2_ON_VECTOR, :], in_=src[:, :, 0:W2_ON_VECTOR, :])
+            nc.scalar.copy(out=dst[:, :, W2_ON_VECTOR:P, :], in_=src[:, :, W2_ON_VECTOR:P, :])
 
         def quantize_w2():
             nc.vector.quantize_mx(out=w2_codes[:].bitcast(FP8X4), scales=w2_scales[:], in_=w2_in[:])
@@ -201,6 +186,9 @@ def tile_gin_pc_kernel(tc, u1, W2_1, b2_1, h, h1, W_out, b_out, out):
             nc.scalar.activation(out=exp_values[:], in_=logits[tile // 2][:, tile % 2, :], func=ACT.Exp,
                                  bias=neg_max[:, tile:tile + 1], scale=1.0, accum_out=exp_sum[:, tile:tile + 1])
 
+        def logarithm(first, last):
+            nc.scalar.activation(out=log_sum[:, first:last], in_=exp_sum[:, first:last], func=ACT.Ln)
+
         def subtract(tile):
             nc.vector.tensor_scalar(out=result[tile // 2][:, tile % 2, :], in0=logits[tile // 2][:, tile % 2, :],
                                     scalar1=neg_max[:, tile:tile + 1], scalar2=log_sum[:, tile:tile + 1],
@@ -210,83 +198,109 @@ def tile_gin_pc_kernel(tc, u1, W2_1, b2_1, h, h1, W_out, b_out, out):
             view = out.rearrange("(p i) c -> p i c", i=TILES)
             nc.sync.dma_start(out=view[:, 2 * j:2 * j + 2, :], in_=result[j][:])
 
+        def stage1_round(j, before, between):
+            for step in before:
+                step()
+            stage1_bias(2 * j)
+            stage1_bias(2 * j + 1)
+            for step in between:
+                step()
+            quantize_h2(j)
+
+        def finish(j):
+            subtract(2 * j)
+            subtract(2 * j + 1)
+            store(j)
+
         load_nodes("u1", 0)
-        load_w2(0)
+        load_w2()
         load_nodes("u1", 1)
-        load_w2(1)
         load_nodes("u1", 2)
         load_biases()
-        load_nodes("u1", 3)
         load_wo(0)
         load_wo(1)
         load_nodes("h", 0)
         load_nodes("h1", 0)
         load_wo(2)
-        for j in range(1, UNITS):
+        load_nodes("h", 1)
+        load_nodes("h1", 1)
+        load_nodes("u1", 3)
+        for j in (2, 3):
             load_nodes("h", j)
             load_nodes("h1", j)
 
-        for n in range(4):
-            spare_plain_pass()
         transpose("u1", 0)
-        spare_plain_pass()
-        interleave_w2(0)
         copy_out("u1", 0)
-        interleave_w2(1)
+        interleave_w2()
         quantize_u1(0)
         quantize_w2()
-        for j in (1, 2):
-            transpose("u1", j)
-            if j == 1:
-                spare_plain_pass()
-            copy_out("u1", j)
-            quantize_u1(j)
-        spread_b_out()
-        spare_plain_pass()
-        transpose("u1", 3)
-        copy_out("u1", 3)
+        transpose("u1", 1)
+        copy_out("u1", 1)
+        quantize_u1(1)
+        transpose("u1", 2)
+        copy_out("u1", 2)
 
-        for j in range(UNITS):
-            stage1_matmuls(2 * j)
-            stage1_matmuls(2 * j + 1)
-            spare_mx_pass()
-            transpose("h", j)
-            transpose("h1", j)
-            stage1_bias(2 * j)
-            stage1_bias(2 * j + 1)
-            if j == 0:
-                quantize_u1(3)
-                interleave_wo(0)
-                interleave_wo(1)
-            elif j == 1:
-                quantize_wo(0, 2)
-                interleave_wo(2)
-            elif j == 2:
-                quantize_wo(2, 3)
-            else:
-                quantize_hh(0)
-            quantize_h2(j)
+        stage1_matmuls(0)
+        stage1_matmuls(1)
+        transpose("h", 0)
+        transpose("h1", 0)
+        stage1_round(0, (), (lambda: quantize_u1(2),))
+        for g in range(3):
+            interleave_wo(g)
+
+        stage1_matmuls(2)
+        stage1_matmuls(3)
+        transpose("h", 1)
+        transpose("h1", 1)
+        stage1_round(1, (), (lambda: quantize_wo(0, 2),))
+        for j in (0, 1):
             copy_out("h", j)
             copy_out("h1", j)
 
-        spare_mx_pass()
-        spare_mx_pass()
+        spread_b_out()
+        stage1_matmuls(4)
+        stage1_matmuls(5)
+        transpose("u1", 3)
+        transpose("h", 2)
+        transpose("h1", 2)
+        stage1_round(2, (lambda: quantize_wo(2, 3),), (lambda: quantize_hh(0),))
+        copy_out("u1", 3)
+        copy_out("h", 2)
+        copy_out("h1", 2)
         quantize_hh(1)
-        for j in range(UNITS):
-            stage2_matmuls(j)
-            if j + 2 < UNITS:
-                quantize_hh(j + 2)
-            if j > 0:
-                row_max(2 * j - 2, 2 * j)
-                exp_and_sum(2 * j - 2)
-                exp_and_sum(2 * j - 1)
+        quantize_u1(3)
+
+        stage2_matmuls(0)
+        stage2_matmuls(1)
+        transpose("h", 3)
+        transpose("h1", 3)
+        for j in (0, 1):
             add_b_out(j)
-        for tile in (TILES - 2, TILES - 1):
+            row_max(2 * j, 2 * j + 2)
+        copy_out("h", 3)
+        copy_out("h1", 3)
+        for tile in range(EARLY_TILES):
+            exp_and_sum(tile)
+        logarithm(0, EARLY_TILES)
+        nc.scalar.activation(out=warm[:, 1:2], in_=log_sum[:, 0:1], func=ACT.Exp)
+
+        stage1_matmuls(6)
+        stage1_matmuls(7)
+        stage1_round(3, (lambda: quantize_hh(2),), (lambda: quantize_hh(3),))
+
+        stage2_matmuls(2)
+        stage2_matmuls(3)
+        add_b_out(2)
+        row_max(4, 6)
+        exp_and_sum(4)
+        exp_and_sum(5)
+        finish(0)
+        add_b_out(3)
+        for tile in (6, 7):
             row_max(tile, tile + 1)
             exp_and_sum(tile)
+        finish(1)
 
-        nc.scalar.activation(out=log_sum[:], in_=exp_sum[:], func=ACT.Ln)
-        for j in range(UNITS):
-            subtract(2 * j)
-            subtract(2 * j + 1)
-            store(j)
+        logarithm(EARLY_TILES, TILES)
+        finish(2)
+        finish(3)

@@ -21,7 +21,6 @@ TILES = NODES // P
 UNITS = TILES // 2
 STAGE1_PSUM = F32
 W2_ON_VECTOR = 84
-EARLY_TILES = 4
 
 
 def tile_gin_pc_kernel(tc, u1, W2_1, b2_1, h, h1, W_out, b_out, out):
@@ -186,9 +185,6 @@ def tile_gin_pc_kernel(tc, u1, W2_1, b2_1, h, h1, W_out, b_out, out):
             nc.scalar.activation(out=exp_values[:], in_=logits[tile // 2][:, tile % 2, :], func=ACT.Exp,
                                  bias=neg_max[:, tile:tile + 1], scale=1.0, accum_out=exp_sum[:, tile:tile + 1])
 
-        def logarithm(first, last):
-            nc.scalar.activation(out=log_sum[:, first:last], in_=exp_sum[:, first:last], func=ACT.Ln)
-
         def subtract(tile):
             nc.vector.tensor_scalar(out=result[tile // 2][:, tile % 2, :], in0=logits[tile // 2][:, tile % 2, :],
                                     scalar1=neg_max[:, tile:tile + 1], scalar2=log_sum[:, tile:tile + 1],
@@ -198,34 +194,18 @@ def tile_gin_pc_kernel(tc, u1, W2_1, b2_1, h, h1, W_out, b_out, out):
             view = out.rearrange("(p i) c -> p i c", i=TILES)
             nc.sync.dma_start(out=view[:, 2 * j:2 * j + 2, :], in_=result[j][:])
 
-        def stage1_round(j, before, between):
-            for step in before:
-                step()
-            stage1_bias(2 * j)
-            stage1_bias(2 * j + 1)
-            for step in between:
-                step()
-            quantize_h2(j)
-
-        def finish(j):
-            subtract(2 * j)
-            subtract(2 * j + 1)
-            store(j)
-
         load_nodes("u1", 0)
         load_w2()
         load_nodes("u1", 1)
         load_nodes("u1", 2)
         load_biases()
+        load_nodes("u1", 3)
         load_wo(0)
         load_wo(1)
         load_nodes("h", 0)
         load_nodes("h1", 0)
         load_wo(2)
-        load_nodes("h", 1)
-        load_nodes("h1", 1)
-        load_nodes("u1", 3)
-        for j in (2, 3):
+        for j in range(1, UNITS):
             load_nodes("h", j)
             load_nodes("h1", j)
 
@@ -234,73 +214,52 @@ def tile_gin_pc_kernel(tc, u1, W2_1, b2_1, h, h1, W_out, b_out, out):
         interleave_w2()
         quantize_u1(0)
         quantize_w2()
-        transpose("u1", 1)
-        copy_out("u1", 1)
-        quantize_u1(1)
-        transpose("u1", 2)
-        copy_out("u1", 2)
+        for j in (1, 2):
+            transpose("u1", j)
+            copy_out("u1", j)
+            quantize_u1(j)
+        spread_b_out()
+        transpose("u1", 3)
+        copy_out("u1", 3)
 
-        stage1_matmuls(0)
-        stage1_matmuls(1)
-        transpose("h", 0)
-        transpose("h1", 0)
-        stage1_round(0, (), (lambda: quantize_u1(2),))
-        for g in range(3):
-            interleave_wo(g)
-
-        stage1_matmuls(2)
-        stage1_matmuls(3)
-        transpose("h", 1)
-        transpose("h1", 1)
-        stage1_round(1, (), (lambda: quantize_wo(0, 2),))
-        for j in (0, 1):
+        for j in range(UNITS):
+            stage1_matmuls(2 * j)
+            stage1_matmuls(2 * j + 1)
+            transpose("h", j)
+            transpose("h1", j)
+            stage1_bias(2 * j)
+            stage1_bias(2 * j + 1)
+            if j == 0:
+                quantize_u1(3)
+                interleave_wo(0)
+                interleave_wo(1)
+            elif j == 1:
+                quantize_wo(0, 2)
+                interleave_wo(2)
+            elif j == 2:
+                quantize_wo(2, 3)
+            else:
+                quantize_hh(0)
+            quantize_h2(j)
             copy_out("h", j)
             copy_out("h1", j)
 
-        spread_b_out()
-        stage1_matmuls(4)
-        stage1_matmuls(5)
-        transpose("u1", 3)
-        transpose("h", 2)
-        transpose("h1", 2)
-        stage1_round(2, (lambda: quantize_wo(2, 3),), (lambda: quantize_hh(0),))
-        copy_out("u1", 3)
-        copy_out("h", 2)
-        copy_out("h1", 2)
         quantize_hh(1)
-        quantize_u1(3)
-
-        stage2_matmuls(0)
-        stage2_matmuls(1)
-        transpose("h", 3)
-        transpose("h1", 3)
-        for j in (0, 1):
+        for j in range(UNITS):
+            stage2_matmuls(j)
+            if j + 2 < UNITS:
+                quantize_hh(j + 2)
+            if j > 0:
+                row_max(2 * j - 2, 2 * j)
+                exp_and_sum(2 * j - 2)
+                exp_and_sum(2 * j - 1)
             add_b_out(j)
-            row_max(2 * j, 2 * j + 2)
-        copy_out("h", 3)
-        copy_out("h1", 3)
-        for tile in range(EARLY_TILES):
-            exp_and_sum(tile)
-        logarithm(0, EARLY_TILES)
-        nc.scalar.activation(out=warm[:, 1:2], in_=log_sum[:, 0:1], func=ACT.Exp)
-
-        stage1_matmuls(6)
-        stage1_matmuls(7)
-        stage1_round(3, (lambda: quantize_hh(2),), (lambda: quantize_hh(3),))
-
-        stage2_matmuls(2)
-        stage2_matmuls(3)
-        add_b_out(2)
-        row_max(4, 6)
-        exp_and_sum(4)
-        exp_and_sum(5)
-        finish(0)
-        add_b_out(3)
-        for tile in (6, 7):
+        for tile in (TILES - 2, TILES - 1):
             row_max(tile, tile + 1)
             exp_and_sum(tile)
-        finish(1)
 
-        logarithm(EARLY_TILES, TILES)
-        finish(2)
-        finish(3)
+        nc.scalar.activation(out=log_sum[:], in_=exp_sum[:], func=ACT.Ln)
+        for j in range(UNITS):
+            subtract(2 * j)
+            subtract(2 * j + 1)
+            store(j)

from contextlib import ExitStack

import concourse.mybir as mybir
from concourse.masks import make_identity

F32 = mybir.dt.float32
BF16 = mybir.dt.bfloat16
U32 = mybir.dt.uint32
U8 = mybir.dt.uint8
FP8X4 = mybir.dt.float8_e4m3fn_x4
ACT = mybir.ActivationFunctionType
ALU = mybir.AluOpType
AX = mybir.AxisListType

NODES, HID, CLASSES = 1024, 512, 256
FLOPS = 2 * NODES * HID * HID + 2 * NODES * 3 * HID * CLASSES

P = 128
PACK = 4
TILES = NODES // P
UNITS = TILES // 2
STAGE1_PSUM = F32
W2_ON_VECTOR = 84


def tile_gin_pc_kernel(tc, u1, W2_1, b2_1, h, h1, W_out, b_out, out):
    nc = tc.nc
    with ExitStack() as ctx:
        keep = ctx.enter_context(tc.tile_pool(name="keep", bufs=1))
        psum = ctx.enter_context(tc.psum_pool(name="psum", bufs=1))
        ctx.enter_context(tc.manual_schedule())

        ident = keep.tile([P, P], F32, name="ident")
        make_identity(nc, ident[:])
        ones = keep.tile([P, P], BF16, name="ones")
        nc.vector.memset(ones[:], 1.0)
        b_out_row = keep.tile([P, CLASSES], BF16, name="b_out_row")
        nc.vector.memset(b_out_row[:], 0.0)
        warm = keep.tile([P, 2], F32, name="warm")
        nc.vector.memset(warm[:], 0.0)
        nc.scalar.activation(out=warm[:, 1:2], in_=warm[:, 0:1], func=ACT.Exp)

        sources = {"u1": u1, "h": h, "h1": h1}
        raw = {}
        for name in sources:
            for j in range(UNITS):
                raw[(name, j)] = keep.tile([P, 2, HID], BF16, name="raw_%s_%d" % (name, j))
        w2_raw = keep.tile([P, PACK, HID], BF16, name="w2_raw")
        wo_raw = [keep.tile([P, PACK, CLASSES], BF16, name="wo_raw%d" % g) for g in range(3)]
        b2 = keep.tile([P, PACK], BF16, name="b2")
        b_out_all = keep.tile([P, CLASSES], F32, name="b_out_all")

        w2_in = keep.tile([P, PACK * HID], BF16, name="w2_in", align_bytes=64)
        w2_codes = keep.tile([P, HID], U32, name="w2_codes", align_bytes=64)
        w2_scales = keep.tile([P, HID], U8, name="w2_scales", align_bytes=64)
        wo_in = keep.tile([P, 3 * PACK * CLASSES], BF16, name="wo_in", align_bytes=64)
        wo_codes = keep.tile([P, 3 * CLASSES], U32, name="wo_codes", align_bytes=64)
        wo_scales = keep.tile([P, 3 * CLASSES], U8, name="wo_scales", align_bytes=64)
        u1_in = [keep.tile([P, 2 * P * PACK], BF16, name="u1_in%d" % j, align_bytes=64) for j in range(UNITS)]
        u1_codes = [keep.tile([P, 2 * P], U32, name="u1_codes%d" % j, align_bytes=64) for j in range(UNITS)]
        u1_scales = [keep.tile([P, 2 * P], U8, name="u1_scales%d" % j, align_bytes=64) for j in range(UNITS)]
        hh_in = [keep.tile([P, 2, 2 * P * PACK], BF16, name="hh_in%d" % j, align_bytes=64) for j in range(UNITS)]
        hh_codes = [keep.tile([P, 4 * P], U32, name="hh_codes%d" % j, align_bytes=64) for j in range(UNITS)]
        hh_scales = [keep.tile([P, 4 * P], U8, name="hh_scales%d" % j, align_bytes=64) for j in range(UNITS)]
        h2_in = [keep.tile([P, 2, P * PACK], BF16, name="h2_in%d" % j, align_bytes=64) for j in range(UNITS)]
        h2_codes = [keep.tile([P, 2 * P], U32, name="h2_codes%d" % j, align_bytes=64) for j in range(UNITS)]
        h2_scales = [keep.tile([P, 2 * P], U8, name="h2_scales%d" % j, align_bytes=64) for j in range(UNITS)]

        logits = [keep.tile([P, 2, CLASSES], F32, name="logits%d" % j) for j in range(UNITS)]
        result = [keep.tile([P, 2, CLASSES], F32, name="result%d" % j) for j in range(UNITS)]
        neg_max = keep.tile([P, TILES], F32, name="neg_max")
        exp_sum = keep.tile([P, TILES], F32, name="exp_sum")
        log_sum = keep.tile([P, TILES], F32, name="log_sum")
        exp_values = keep.tile([P, CLASSES], BF16, name="exp_values")

        banks = {}

        def load_nodes(name, j):
            view = sources[name].rearrange("(p i) k -> p i k", i=TILES)
            nc.sync.dma_start(out=raw[(name, j)][:], in_=view[:, 2 * j:2 * j + 2, :])

        def load_w2():
            nc.sync.dma_start(out=w2_raw[:], in_=W2_1.rearrange("(p t) c -> p t c", t=PACK))

        def load_wo(g):
            rows = W_out[HID * g:HID * (g + 1), :]
            nc.sync.dma_start(out=wo_raw[g][:], in_=rows.rearrange("(p t) c -> p t c", t=PACK))

        def load_biases():
            nc.sync.dma_start(out=b2[:], in_=b2_1.rearrange("(p t) -> p t", t=PACK))
            nc.sync.dma_start(out=b_out_row[0:1, :], in_=b_out.unsqueeze(0))

        def interleave_w2():
            dst = w2_in[:].rearrange("p (s m t) -> p s m t", s=PACK, t=PACK)
            src = w2_raw[:].rearrange("p t (m s) -> p s m t", s=PACK)
            nc.vector.tensor_copy(out=dst[:, :, 0:W2_ON_VECTOR, :], in_=src[:, :, 0:W2_ON_VECTOR, :])
            nc.scalar.copy(out=dst[:, :, W2_ON_VECTOR:P, :], in_=src[:, :, W2_ON_VECTOR:P, :])

        def quantize_w2():
            nc.vector.quantize_mx(out=w2_codes[:].bitcast(FP8X4), scales=w2_scales[:], in_=w2_in[:])

        def interleave_wo(g):
            width = PACK * CLASSES
            nc.scalar.copy(out=wo_in[:, width * g:width * (g + 1)].rearrange("p (c t) -> p c t", t=PACK),
                           in_=wo_raw[g][:].rearrange("p t c -> p c t"))

        def quantize_wo(g0, g1):
            nc.vector.quantize_mx(out=wo_codes[:, CLASSES * g0:CLASSES * g1].bitcast(FP8X4),
                                  scales=wo_scales[:, CLASSES * g0:CLASSES * g1],
                                  in_=wo_in[:, PACK * CLASSES * g0:PACK * CLASSES * g1])

        def spread_b_out():
            bank = psum.tile([P, 2, CLASSES], F32, name="spread", tag="logits", bufs=2)
            nc.tensor.matmul(out=bank[:, 0, :], lhsT=ones[:], rhs=b_out_row[:], start=True, stop=True)
            nc.scalar.copy(out=b_out_all[:], in_=bank[:, 0, :])

        def transpose(name, j):
            words = raw[(name, j)][:].bitcast(F32)
            bank = psum.tile([P, 2, 2, P], F32, name="turned", tag="turned", bufs=4)
            banks[(name, j)] = bank
            for i in range(2):
                for u in range(2):
                    nc.tensor.transpose(bank[:, i, u, :], words[:, i, u:HID // 2:2], ident[:])

        def copy_out(name, j):
            dst = u1_in[j][:] if name == "u1" else hh_in[j][:, 0 if name == "h" else 1, :]
            nc.scalar.copy(out=dst.bitcast(F32).rearrange("p (i r u) -> p i r u", i=2, u=2),
                           in_=banks[(name, j)][:].rearrange("p i u r -> p i r u"))

        def quantize_u1(j):
            nc.vector.quantize_mx(out=u1_codes[j][:].bitcast(FP8X4), scales=u1_scales[j][:], in_=u1_in[j][:])

        def quantize_hh(j):
            nc.vector.quantize_mx(out=hh_codes[j][:].bitcast(FP8X4), scales=hh_scales[j][:],
                                  in_=hh_in[j][:].rearrange("p x c -> p (x c)"))

        def stage1_matmuls(tile):
            j, i = tile // 2, tile % 2
            nodes = slice(P * i, P * (i + 1))
            bank = psum.tile([P, PACK, P], STAGE1_PSUM, name="stage1", tag="stage1", bufs=2)
            banks[("h2", tile)] = bank
            for s in range(PACK):
                block = slice(P * s, P * (s + 1))
                nc.tensor.matmul_mx(out=bank[:, s, :],
                                    lhsT=w2_codes[:, block].bitcast(FP8X4), lhsT_scale=w2_scales[:, block],
                                    rhs=u1_codes[j][:, nodes].bitcast(FP8X4), rhs_scale=u1_scales[j][:, nodes],
                                    start=True, stop=True)

        def stage1_bias(tile):
            j, i = tile // 2, tile % 2
            nc.vector.tensor_tensor(out=h2_in[j][:, i, :].rearrange("p (n s) -> p n s", s=PACK),
                                    in0=banks[("h2", tile)][:].rearrange("p s n -> p n s"),
                                    in1=b2[:].unsqueeze(1).to_broadcast([P, P, PACK]), op=ALU.add)

        def quantize_h2(j):
            nc.vector.quantize_mx(out=h2_codes[j][:].bitcast(FP8X4), scales=h2_scales[j][:],
                                  in_=h2_in[j][:].rearrange("p i c -> p (i c)"))

        def stage2_matmuls(j):
            bank = psum.tile([P, 2, CLASSES], F32, name="logits", tag="logits", bufs=2)
            banks[("logits", j)] = bank
            for i in range(2):
                passes = ((hh_codes[j], hh_scales[j], P * i),
                          (hh_codes[j], hh_scales[j], 2 * P + P * i),
                          (h2_codes[j], h2_scales[j], P * i))
                for g in range(3):
                    codes, scales, first = passes[g]
                    nc.tensor.matmul_mx(out=bank[:, i, :],
                                        lhsT=codes[:, first:first + P].bitcast(FP8X4),
                                        lhsT_scale=scales[:, first:first + P],
                                        rhs=wo_codes[:, CLASSES * g:CLASSES * (g + 1)].bitcast(FP8X4),
                                        rhs_scale=wo_scales[:, CLASSES * g:CLASSES * (g + 1)],
                                        start=(g == 0), stop=(g == 2))

        def add_b_out(j):
            nc.vector.tensor_tensor(out=logits[j][:], in0=banks[("logits", j)][:],
                                    in1=b_out_all[:].unsqueeze(1).to_broadcast([P, 2, CLASSES]), op=ALU.add)

        def row_max(first, last):
            j = first // 2
            nc.vector.tensor_reduce(out=neg_max[:, first:last], in_=logits[j][:, first - 2 * j:last - 2 * j, :],
                                    axis=AX.X, op=ALU.max, negate=True)

        def exp_and_sum(tile):
            nc.scalar.activation(out=exp_values[:], in_=logits[tile // 2][:, tile % 2, :], func=ACT.Exp,
                                 bias=neg_max[:, tile:tile + 1], scale=1.0, accum_out=exp_sum[:, tile:tile + 1])

        def subtract(tile):
            nc.vector.tensor_scalar(out=result[tile // 2][:, tile % 2, :], in0=logits[tile // 2][:, tile % 2, :],
                                    scalar1=neg_max[:, tile:tile + 1], scalar2=log_sum[:, tile:tile + 1],
                                    op0=ALU.add, op1=ALU.subtract)

        def store(j):
            view = out.rearrange("(p i) c -> p i c", i=TILES)
            nc.sync.dma_start(out=view[:, 2 * j:2 * j + 2, :], in_=result[j][:])

        load_nodes("u1", 0)
        load_w2()
        load_nodes("u1", 1)
        load_nodes("u1", 2)
        load_biases()
        load_nodes("u1", 3)
        load_wo(0)
        load_wo(1)
        load_nodes("h", 0)
        load_nodes("h1", 0)
        load_wo(2)
        for j in range(1, UNITS):
            load_nodes("h", j)
            load_nodes("h1", j)

        transpose("u1", 0)
        copy_out("u1", 0)
        interleave_w2()
        quantize_u1(0)
        quantize_w2()
        for j in (1, 2):
            transpose("u1", j)
            copy_out("u1", j)
            quantize_u1(j)
        spread_b_out()
        transpose("u1", 3)
        copy_out("u1", 3)

        for j in range(UNITS):
            stage1_matmuls(2 * j)
            stage1_matmuls(2 * j + 1)
            transpose("h", j)
            transpose("h1", j)
            stage1_bias(2 * j)
            stage1_bias(2 * j + 1)
            if j == 0:
                quantize_u1(3)
                interleave_wo(0)
                interleave_wo(1)
            elif j == 1:
                quantize_wo(0, 2)
                interleave_wo(2)
            elif j == 2:
                quantize_wo(2, 3)
            else:
                quantize_hh(0)
            quantize_h2(j)
            copy_out("h", j)
            copy_out("h1", j)

        quantize_hh(1)
        for j in range(UNITS):
            stage2_matmuls(j)
            if j + 2 < UNITS:
                quantize_hh(j + 2)
            if j > 0:
                row_max(2 * j - 2, 2 * j)
                exp_and_sum(2 * j - 2)
                exp_and_sum(2 * j - 1)
            add_b_out(j)
        for tile in (TILES - 2, TILES - 1):
            row_max(tile, tile + 1)
            exp_and_sum(tile)

        nc.scalar.activation(out=log_sum[:], in_=exp_sum[:], func=ACT.Ln)
        for j in range(UNITS):
            subtract(2 * j)
            subtract(2 * j + 1)
            store(j)
